import numpy as np
import ml_dtypes

BF16 = ml_dtypes.bfloat16


def bf(x):
    return np.asarray(x, np.float32).astype(BF16)


def f32(x):
    return np.asarray(x, np.float32)


def f64(x):
    return np.asarray(x).astype(np.float64)


def striped(idx):
    return np.tile(idx.reshape(-1, 16).T, (8, 1))


C, H, S, N = 256, 128, 1024, 512
ERF_LIM, ERF_TERMS = 6.0, 150
LORA_SCALE, BIAS_SCALE = 2.0, 0.2


def erf(a):
    c = np.clip(a, -ERF_LIM, ERF_LIM)
    term = c.copy()
    tot = c.copy()
    for n in range(1, ERF_TERMS):
        term = term * (2.0 * c * c) / (2.0 * n + 1.0)
        tot = tot + term
    return np.where(np.abs(a) > ERF_LIM, np.sign(a), 2.0 / np.sqrt(np.pi) * np.exp(-c * c) * tot)


def gelu_erf(v):
    return 0.5 * v * (1.0 + erf(v / np.sqrt(2.0)))


def setup_inputs():
    return {"h": f32(np.random.standard_normal((H, N))), "lora": f32(LORA_SCALE * np.random.standard_normal((C, S))), "lorab": f32(LORA_SCALE * np.random.standard_normal((C, 1))), "w": bf(np.random.standard_normal((H, H)) / np.sqrt(H)), "b": f32(BIAS_SCALE * np.random.standard_normal((H, 1))), "offs": striped(np.random.permutation(S)[:N])}


def reference(h, lora, lorab, w, b, offs):
    idx = offs[:16].T.reshape(-1)
    x = gelu_erf(f64(h))
    tab = f64(lora) + f64(lorab)
    p = tab[H:, idx] * x
    m = p.sum(axis=0, keepdims=True) / H
    z = tab[:H, idx] * m
    return gelu_erf(f64(w).T @ x + f64(b) + z)

@@ -1,0 +1,95 @@
+import concourse.mybir as mybir
+
+F32, BF16, U16 = mybir.dt.float32, mybir.dt.bfloat16, mybir.dt.uint16
+ACT = mybir.ActivationFunctionType
+ALU = mybir.AluOpType
+
+P = 128
+S = 1024
+N = 512
+PER_COLUMN = 16
+
+PIECES = 4
+PIECE = N // PIECES
+PIECE_COLUMNS = PIECE // PER_COLUMN
+HALF = S // 2
+
+FLOPS = 2 * P * P * N + 2 * P * N + 2 * P * N
+BYTES = 4 * P * N + 4 * 2 * P * N + 4 * 2 * P + 2 * P * P + 4 * P + 2 * P * (N // PER_COLUMN) + 4 * P * N
+
+
+def tile_multisubjectniirfpeft_kernel(tc, h, lora, lorab, w, b, offs, out):
+    nc = tc.nc
+    halves = [slice(0, HALF), slice(HALF, S)]
+    vector_share, scalar_share = slice(HALF, HALF + 352), slice(HALF + 352, S)
+    pieces = [slice(i * PIECE, (i + 1) * PIECE) for i in range(PIECES)]
+    with (
+        tc.tile_pool(name="held", bufs=1) as held,
+        tc.tile_pool(name="ring", bufs=3) as ring,
+        tc.psum_pool(name="psum", bufs=1) as psum,
+    ):
+        h_sb = held.tile([P, N], F32, name="h_sb")
+        nc.sync.dma_start(h_sb[:], h)
+        lora_in = held.tile([P, S], F32, name="lora_in")
+        for half in halves:
+            nc.sync.dma_start(lora_in[:, half], lora[P : 2 * P, half])
+        offsets = held.tile([P, N // PER_COLUMN], U16, name="offsets")
+        nc.sync.dma_start(offsets[:], offs)
+        w_sb = held.tile([P, P], BF16, name="w_sb")
+        nc.sync.dma_start(w_sb[:], w)
+        lora_out = held.tile([P, S], F32, name="lora_out")
+        for half in halves:
+            nc.sync.dma_start(lora_out[:, half], lora[0:P, half])
+        b_sb = held.tile([P, 1], F32, name="b_sb")
+        nc.sync.dma_start(b_sb[:], b)
+        biases = held.tile([P, 2], F32, name="biases")
+        nc.scalar.dma_start(biases[:], lorab.rearrange("(a p) o -> p (a o)", p=P))
+        bias_out, bias_in = biases[:, 0:1], biases[:, 1:2]
+
+        mean_w = held.tile([P, P], BF16, name="mean_w")
+        nc.vector.memset(mean_w[:], 1.0 / P)
+
+        x = held.tile([P, N], F32, name="x")
+        nc.scalar.activation(x[:], h_sb[:], ACT.Gelu)
+        x_bf = held.tile([P, N], BF16, name="x_bf")
+        nc.scalar.activation(x_bf[:], h_sb[:], ACT.Gelu)
+        wx_ps = psum.tile([P, N], F32, name="wx_ps")
+        nc.tensor.matmul(wx_ps[:], w_sb[:], x_bf[:], start=True, stop=True)
+
+        tab_in = held.tile([P, S], F32, name="tab_in")
+        tab_out = held.tile([P, S], F32, name="tab_out")
+        nc.vector.tensor_scalar_add(tab_in[:, halves[0]], lora_in[:, halves[0]], bias_in)
+        nc.vector.tensor_scalar_add(tab_in[:, vector_share], lora_in[:, vector_share], bias_in)
+        nc.scalar.activation(
+            tab_in[:, scalar_share], lora_in[:, scalar_share], ACT.Identity, bias=bias_in
+        )
+        nc.scalar.activation(
+            tab_out[:, halves[0]], lora_out[:, halves[0]], ACT.Identity, bias=bias_out
+        )
+
+        p = held.tile([P, N], F32, name="p")
+        m_ps = [psum.tile([P, PIECE], F32, name=f"m_ps{i}") for i in range(PIECES)]
+        m = held.tile([P, N], F32, name="m")
+        for i, cols in enumerate(pieces):
+            picked = tab_in[:].indirect(offsets[:, i * PIECE_COLUMNS : (i + 1) * PIECE_COLUMNS])
+            nc.vector.tensor_tensor(p[:, cols], picked, x[:, cols], ALU.mult)
+            p_bf = ring.tile([P, PIECE], BF16, name="p_bf")
+            nc.scalar.copy(p_bf[:], p[:, cols])
+            nc.tensor.matmul(m_ps[i][:], mean_w[:], p_bf[:], start=True, stop=True)
+            nc.scalar.copy(m[:, cols], m_ps[i][:])
+
+        nc.vector.tensor_scalar_add(tab_out[:, halves[1]], lora_out[:, halves[1]], bias_out)
+
+        z = held.tile([P, N], F32, name="z")
+        y = held.tile([P, N], F32, name="y")
+        out_sb = held.tile([P, N], F32, name="out_sb")
+        for i in range(PIECES + 1):
+            if i < PIECES:
+                cols = pieces[i]
+                picked = tab_out[:].indirect(offsets[:, i * PIECE_COLUMNS : (i + 1) * PIECE_COLUMNS])
+                nc.vector.tensor_tensor(z[:, cols], picked, m[:, cols], ALU.mult)
+            if i > 0:
+                cols = pieces[i - 1]
+                nc.vector.tensor_tensor(y[:, cols], wx_ps[:, cols], z[:, cols], ALU.add)
+                nc.scalar.activation(out_sb[:, cols], y[:, cols], ACT.Gelu, bias=b_sb[:, 0:1])
+                nc.sync.dma_start(out[:, cols], out_sb[:, cols])

@@ -21,7 +21,9 @@ BYTES = 4 * P * N + 4 * 2 * P * N + 4 * 2 * P + 2 * P * P + 4 * P + 2 * P * (N /
 def tile_multisubjectniirfpeft_kernel(tc, h, lora, lorab, w, b, offs, out):
     nc = tc.nc
     halves = [slice(0, HALF), slice(HALF, S)]
-    vector_share, scalar_share = slice(HALF, HALF + 352), slice(HALF + 352, S)
+    in_vector, in_scalar = slice(HALF, HALF + 352), slice(HALF + 352, S)
+    out_scalar, out_vector = slice(0, 352), slice(352, S)
+    h_halves = [slice(0, N // 2), slice(N // 2, N)]
     pieces = [slice(i * PIECE, (i + 1) * PIECE) for i in range(PIECES)]
     with (
         tc.tile_pool(name="held", bufs=1) as held,
@@ -29,42 +31,43 @@ def tile_multisubjectniirfpeft_kernel(tc, h, lora, lorab, w, b, offs, out):
         tc.psum_pool(name="psum", bufs=1) as psum,
     ):
         h_sb = held.tile([P, N], F32, name="h_sb")
-        nc.sync.dma_start(h_sb[:], h)
+        nc.sync.dma_start(h_sb[:, h_halves[0]], h[:, h_halves[0]])
         lora_in = held.tile([P, S], F32, name="lora_in")
         for half in halves:
             nc.sync.dma_start(lora_in[:, half], lora[P : 2 * P, half])
         offsets = held.tile([P, N // PER_COLUMN], U16, name="offsets")
         nc.sync.dma_start(offsets[:], offs)
-        w_sb = held.tile([P, P], BF16, name="w_sb")
-        nc.sync.dma_start(w_sb[:], w)
+        nc.sync.dma_start(h_sb[:, h_halves[1]], h[:, h_halves[1]])
         lora_out = held.tile([P, S], F32, name="lora_out")
-        for half in halves:
-            nc.sync.dma_start(lora_out[:, half], lora[0:P, half])
+        for part in (out_scalar, out_vector):
+            nc.sync.dma_start(lora_out[:, part], lora[0:P, part])
         b_sb = held.tile([P, 1], F32, name="b_sb")
         nc.sync.dma_start(b_sb[:], b)
         biases = held.tile([P, 2], F32, name="biases")
         nc.scalar.dma_start(biases[:], lorab.rearrange("(a p) o -> p (a o)", p=P))
         bias_out, bias_in = biases[:, 0:1], biases[:, 1:2]
+        w_sb = held.tile([P, P], BF16, name="w_sb")
+        nc.scalar.dma_start(w_sb[:], w)
 
         mean_w = held.tile([P, P], BF16, name="mean_w")
         nc.vector.memset(mean_w[:], 1.0 / P)
 
         x = held.tile([P, N], F32, name="x")
-        nc.scalar.activation(x[:], h_sb[:], ACT.Gelu)
         x_bf = held.tile([P, N], BF16, name="x_bf")
-        nc.scalar.activation(x_bf[:], h_sb[:], ACT.Gelu)
         wx_ps = psum.tile([P, N], F32, name="wx_ps")
-        nc.tensor.matmul(wx_ps[:], w_sb[:], x_bf[:], start=True, stop=True)
+        for cols in h_halves:
+            nc.scalar.activation(x[:, cols], h_sb[:, cols], ACT.Gelu)
+            nc.scalar.activation(x_bf[:, cols], h_sb[:, cols], ACT.Gelu)
+            nc.tensor.matmul(wx_ps[:, cols], w_sb[:], x_bf[:, cols], start=True, stop=True)
 
         tab_in = held.tile([P, S], F32, name="tab_in")
         tab_out = held.tile([P, S], F32, name="tab_out")
         nc.vector.tensor_scalar_add(tab_in[:, halves[0]], lora_in[:, halves[0]], bias_in)
-        nc.vector.tensor_scalar_add(tab_in[:, vector_share], lora_in[:, vector_share], bias_in)
+        nc.vector.tensor_scalar_add(tab_in[:, in_vector], lora_in[:, in_vector], bias_in)
+        nc.scalar.activation(tab_in[:, in_scalar], lora_in[:, in_scalar], ACT.Identity, bias=bias_in)
+
         nc.scalar.activation(
-            tab_in[:, scalar_share], lora_in[:, scalar_share], ACT.Identity, bias=bias_in
-        )
-        nc.scalar.activation(
-            tab_out[:, halves[0]], lora_out[:, halves[0]], ACT.Identity, bias=bias_out
+            tab_out[:, out_scalar], lora_out[:, out_scalar], ACT.Identity, bias=bias_out
         )
 
         p = held.tile([P, N], F32, name="p")
@@ -78,7 +81,7 @@ def tile_multisubjectniirfpeft_kernel(tc, h, lora, lorab, w, b, offs, out):
             nc.tensor.matmul(m_ps[i][:], mean_w[:], p_bf[:], start=True, stop=True)
             nc.scalar.copy(m[:, cols], m_ps[i][:])
 
-        nc.vector.tensor_scalar_add(tab_out[:, halves[1]], lora_out[:, halves[1]], bias_out)
+        nc.vector.tensor_scalar_add(tab_out[:, out_vector], lora_out[:, out_vector], bias_out)
 
         z = held.tile([P, N], F32, name="z")
         y = held.tile([P, N], F32, name="y")

import concourse.mybir as mybir

F32, BF16, U16 = mybir.dt.float32, mybir.dt.bfloat16, mybir.dt.uint16
ACT = mybir.ActivationFunctionType
ALU = mybir.AluOpType

P = 128
S = 1024
N = 512
PER_COLUMN = 16

PIECES = 4
PIECE = N // PIECES
PIECE_COLUMNS = PIECE // PER_COLUMN
HALF = S // 2

FLOPS = 2 * P * P * N + 2 * P * N + 2 * P * N
BYTES = 4 * P * N + 4 * 2 * P * N + 4 * 2 * P + 2 * P * P + 4 * P + 2 * P * (N // PER_COLUMN) + 4 * P * N


def tile_multisubjectniirfpeft_kernel(tc, h, lora, lorab, w, b, offs, out):
    nc = tc.nc
    halves = [slice(0, HALF), slice(HALF, S)]
    in_vector, in_scalar = slice(HALF, HALF + 352), slice(HALF + 352, S)
    out_scalar, out_vector = slice(0, 352), slice(352, S)
    h_halves = [slice(0, N // 2), slice(N // 2, N)]
    pieces = [slice(i * PIECE, (i + 1) * PIECE) for i in range(PIECES)]
    with (
        tc.tile_pool(name="held", bufs=1) as held,
        tc.tile_pool(name="ring", bufs=3) as ring,
        tc.psum_pool(name="psum", bufs=1) as psum,
    ):
        h_sb = held.tile([P, N], F32, name="h_sb")
        nc.sync.dma_start(h_sb[:, h_halves[0]], h[:, h_halves[0]])
        lora_in = held.tile([P, S], F32, name="lora_in")
        for half in halves:
            nc.sync.dma_start(lora_in[:, half], lora[P : 2 * P, half])
        offsets = held.tile([P, N // PER_COLUMN], U16, name="offsets")
        nc.sync.dma_start(offsets[:], offs)
        nc.sync.dma_start(h_sb[:, h_halves[1]], h[:, h_halves[1]])
        lora_out = held.tile([P, S], F32, name="lora_out")
        for part in (out_scalar, out_vector):
            nc.sync.dma_start(lora_out[:, part], lora[0:P, part])
        b_sb = held.tile([P, 1], F32, name="b_sb")
        nc.sync.dma_start(b_sb[:], b)
        biases = held.tile([P, 2], F32, name="biases")
        nc.scalar.dma_start(biases[:], lorab.rearrange("(a p) o -> p (a o)", p=P))
        bias_out, bias_in = biases[:, 0:1], biases[:, 1:2]
        w_sb = held.tile([P, P], BF16, name="w_sb")
        nc.scalar.dma_start(w_sb[:], w)

        mean_w = held.tile([P, P], BF16, name="mean_w")
        nc.vector.memset(mean_w[:], 1.0 / P)

        x = held.tile([P, N], F32, name="x")
        x_bf = held.tile([P, N], BF16, name="x_bf")
        wx_ps = psum.tile([P, N], F32, name="wx_ps")
        for cols in h_halves:
            nc.scalar.activation(x[:, cols], h_sb[:, cols], ACT.Gelu)
            nc.scalar.activation(x_bf[:, cols], h_sb[:, cols], ACT.Gelu)
            nc.tensor.matmul(wx_ps[:, cols], w_sb[:], x_bf[:, cols], start=True, stop=True)

        tab_in = held.tile([P, S], F32, name="tab_in")
        tab_out = held.tile([P, S], F32, name="tab_out")
        nc.vector.tensor_scalar_add(tab_in[:, halves[0]], lora_in[:, halves[0]], bias_in)
        nc.vector.tensor_scalar_add(tab_in[:, in_vector], lora_in[:, in_vector], bias_in)
        nc.scalar.activation(tab_in[:, in_scalar], lora_in[:, in_scalar], ACT.Identity, bias=bias_in)

        nc.scalar.activation(
            tab_out[:, out_scalar], lora_out[:, out_scalar], ACT.Identity, bias=bias_out
        )

        p = held.tile([P, N], F32, name="p")
        m_ps = [psum.tile([P, PIECE], F32, name=f"m_ps{i}") for i in range(PIECES)]
        m = held.tile([P, N], F32, name="m")
        for i, cols in enumerate(pieces):
            picked = tab_in[:].indirect(offsets[:, i * PIECE_COLUMNS : (i + 1) * PIECE_COLUMNS])
            nc.vector.tensor_tensor(p[:, cols], picked, x[:, cols], ALU.mult)
            p_bf = ring.tile([P, PIECE], BF16, name="p_bf")
            nc.scalar.copy(p_bf[:], p[:, cols])
            nc.tensor.matmul(m_ps[i][:], mean_w[:], p_bf[:], start=True, stop=True)
            nc.scalar.copy(m[:, cols], m_ps[i][:])

        nc.vector.tensor_scalar_add(tab_out[:, out_vector], lora_out[:, out_vector], bias_out)

        z = held.tile([P, N], F32, name="z")
        y = held.tile([P, N], F32, name="y")
        out_sb = held.tile([P, N], F32, name="out_sb")
        for i in range(PIECES + 1):
            if i < PIECES:
                cols = pieces[i]
                picked = tab_out[:].indirect(offsets[:, i * PIECE_COLUMNS : (i + 1) * PIECE_COLUMNS])
                nc.vector.tensor_tensor(z[:, cols], picked, m[:, cols], ALU.mult)
            if i > 0:
                cols = pieces[i - 1]
                nc.vector.tensor_tensor(y[:, cols], wx_ps[:, cols], z[:, cols], ALU.add)
                nc.scalar.activation(out_sb[:, cols], y[:, cols], ACT.Gelu, bias=b_sb[:, 0:1])
                nc.sync.dma_start(out[:, cols], out_sb[:, cols])
